import numpy as np
import ml_dtypes


def mxq(x, axis, fmt="e4m3"):
    dtype, down = {"e4m3": (ml_dtypes.float8_e4m3fn, 7), "e5m2": (ml_dtypes.float8_e5m2, 14)}[fmt]
    v = np.moveaxis(np.asarray(x, np.float32).astype(ml_dtypes.bfloat16).astype(np.float64), axis, -1)
    blocks = v.reshape(v.shape[:-1] + (-1, 32))
    amax = np.abs(blocks).max(-1, keepdims=True)
    byte = np.maximum(np.where(amax > 0, np.frexp(amax)[1] - 1 + 127, 0) - down, 1)
    scale = np.exp2(byte - 127.0)
    codes = (blocks / scale).astype(np.float32).astype(dtype).astype(np.float64)
    return np.moveaxis((codes * scale).reshape(v.shape), -1, axis)


BF16 = ml_dtypes.bfloat16


def bf(x):
    return np.asarray(x, np.float32).astype(BF16)


def f64(x):
    return np.asarray(x).astype(np.float64)


B, C_IN, C_OUT, H, W = 2, 512, 512, 32, 32
SC = 1.0 / np.sqrt(np.sqrt(C_IN))


def sign_ste(v, alpha):
    est = np.tanh(alpha * v)
    return (np.sign(v) - est) + est


def setup_inputs():
    return {"x": bf(np.random.standard_normal((B, C_IN, H, W)) * SC),
            "weight": bf(np.random.standard_normal((C_OUT, C_IN, 1, 1)) * SC),
            "alpha_x": bf(1.0 + 0.1 * np.random.standard_normal(1)),
            "alpha_w": bf(1.0 + 0.1 * np.random.standard_normal(1))}


def reference(x, weight, alpha_x, alpha_w):
    x, weight, alpha_x, alpha_w = f64(x), f64(weight), f64(alpha_x), f64(alpha_w)
    b, c, h, w = x.shape
    out_ch = weight.shape[0]
    x_unf = x.reshape(b, c, h * w).transpose(0, 2, 1)
    w_unf = weight.reshape(out_ch, c).T
    signxw = mxq(sign_ste(x_unf, alpha_x), 2, "e4m3") @ mxq(w_unf, 0, "e4m3")
    signwx = mxq(x_unf, 2, "e4m3") @ mxq(sign_ste(w_unf, alpha_w), 0, "e4m3")
    return (signxw + signwx).transpose(0, 2, 1).reshape(b, out_ch, h, w)

@@ -1,0 +1,198 @@
+import concourse.mybir as mybir
+from concourse.masks import make_identity
+
+FLOPS = 2 * 2 * 2 * 1024 * 512 * 512
+
+BF16 = mybir.dt.bfloat16
+F32 = mybir.dt.float32
+U32 = mybir.dt.uint32
+U8 = mybir.dt.uint8
+FP8X4 = mybir.dt.float8_e4m3fn_x4
+ALU = mybir.AluOpType
+ACT = mybir.ActivationFunctionType
+
+P = 128
+PACK = 4
+N_TILE = 512
+CHUNKS = 4
+BLOCKS = 4
+TINY = 2.0 ** -133
+UP_A = 2.0 ** 67
+UP_B = 2.0 ** 66
+
+SCALAR_SIGN_COLS = (512, 128, 128, 96)
+EXIT = ("ssss", "ssss", "ssss", "svsv")
+
+
+def by_fours(grouped_ap, rows_ap):
+    return (
+        grouped_ap.rearrange("p (c i) t -> p c t i", i=4),
+        rows_ap.rearrange("p t (c i) -> p c t i", i=4),
+    )
+
+
+def tile_pointwise_kernel(tc, x, weight, alpha_x, alpha_w, out):
+    nc = tc.nc
+    with tc.tile_pool(name="keep", bufs=1) as keep, tc.psum_pool(name="psum", bufs=8) as psum:
+        raw = []
+        w_sb = keep.tile([P, BLOCKS * 512], BF16, name="w_sb")
+        for c in range(CHUNKS):
+            b, half = divmod(c, 2)
+            r = keep.tile([P, PACK, N_TILE], BF16, name="raw%d" % c)
+            raw.append(r)
+            nc.sync.dma_start(
+                out=r[:],
+                in_=x[b].rearrange("(p j) h w -> p j (h w)", j=PACK)[:, :, half * N_TILE : (half + 1) * N_TILE],
+            )
+            if c == 0:
+                nc.sync.dma_start(out=w_sb[:], in_=weight.rearrange("(p ob) c a b -> p (ob c a b)", ob=BLOCKS))
+
+        ident = keep.tile([P, P], F32, name="ident")
+        make_identity(nc, ident[:])
+
+        xg = [keep.tile([P, N_TILE, PACK], BF16, name="xg%d" % c, align_bytes=64) for c in range(CHUNKS)]
+        sg = [keep.tile([P, N_TILE, PACK], BF16, name="sg%d" % c, align_bytes=64) for c in range(CHUNKS)]
+        tmp = [keep.tile([P, N_TILE, PACK], BF16, name="tmp%d" % c, align_bytes=64) for c in range(CHUNKS)]
+        xq = [keep.tile([P, N_TILE], U32, name="xq%d" % c, align_bytes=64) for c in range(CHUNKS)]
+        xs = [keep.tile([P, N_TILE], U8, name="xs%d" % c, align_bytes=64) for c in range(CHUNKS)]
+        sq = [keep.tile([P, N_TILE], U32, name="sq%d" % c, align_bytes=64) for c in range(CHUNKS)]
+        ss = [keep.tile([P, N_TILE], U8, name="ss%d" % c, align_bytes=64) for c in range(CHUNKS)]
+        res = [keep.tile([P, BLOCKS, N_TILE], F32, name="res%d" % c) for c in range(CHUNKS)]
+
+        wg = keep.tile([P, BLOCKS * P * PACK], BF16, name="wg", align_bytes=64)
+        swg = keep.tile([P, BLOCKS * P * PACK], BF16, name="swg", align_bytes=64)
+        wtmp = keep.tile([P, BLOCKS * P * PACK], BF16, name="wtmp", align_bytes=64)
+        wq = keep.tile([P, BLOCKS * P], U32, name="wq", align_bytes=64)
+        ws = keep.tile([P, BLOCKS * P], U8, name="ws", align_bytes=64)
+        swq = keep.tile([P, BLOCKS * P], U32, name="swq", align_bytes=64)
+        sws = keep.tile([P, BLOCKS * P], U8, name="sws", align_bytes=64)
+
+        def quantise(codes, scales, values):
+            nc.vector.quantize_mx(out=codes.bitcast(FP8X4), scales=scales, in_=values)
+
+        def vector_sign_1(dst, src):
+            nc.vector.tensor_scalar(out=dst, in0=src, scalar1=-TINY, scalar2=TINY, op0=ALU.max, op1=ALU.min)
+
+        def vector_sign_2(dst, src):
+            nc.vector.tensor_scalar(out=dst, in0=src, scalar1=UP_A, scalar2=UP_B, op0=ALU.mult, op1=ALU.mult)
+
+        def regroup(c):
+            dst, src = by_fours(xg[c][:], raw[c][:])
+            nc.vector.tensor_copy(out=dst, in_=src)
+
+        def scalar_sign(c):
+            n = SCALAR_SIGN_COLS[c]
+            if n:
+                dst, src = by_fours(sg[c][:, :n, :], raw[c][:, :, :n])
+                nc.scalar.activation(out=dst, in_=src, func=ACT.Sign)
+
+        def flat(t, c, lo):
+            return t[c][:, lo:, :].rearrange("p w j -> p (w j)")
+
+        def sign_1(c):
+            n = SCALAR_SIGN_COLS[c]
+            if n < N_TILE:
+                vector_sign_1(flat(tmp, c, n), flat(xg, c, n))
+
+        def sign_2(c):
+            n = SCALAR_SIGN_COLS[c]
+            if n < N_TILE:
+                vector_sign_2(flat(sg, c, n), flat(tmp, c, n))
+
+        def quantise_x(c):
+            quantise(xq[c][:], xs[c][:], flat(xg, c, 0))
+
+        def quantise_s(c):
+            quantise(sq[c][:], ss[c][:], flat(sg, c, 0))
+
+        w_words = w_sb[:].bitcast(F32).rearrange("p (ob q u) -> p ob q u", ob=BLOCKS, u=2)
+        wg_words = wg[:].bitcast(F32).rearrange("p (ob m u) -> p ob m u", ob=BLOCKS, u=2)
+        HALF = 2 * P * PACK
+
+        regroup(0)
+        scalar_sign(0)
+        wt = []
+        for pair in range(2):
+            pt = psum.tile([P, 2, 2, P], F32, tag="bank", name="wt%d" % pair)
+            wt.append(pt)
+            for i in range(2):
+                for u in range(2):
+                    nc.tensor.transpose(pt[:, i, u, :], w_words[:, 2 * pair + i, :, u], ident[:])
+        quantise_x(0)
+        nc.vector.tensor_copy(out=wg_words[:, 0:2], in_=wt[0][:].rearrange("p i u m -> p i m u"))
+        nc.scalar.copy(out=wg_words[:, 2:4], in_=wt[1][:].rearrange("p i u m -> p i m u"))
+        quantise(wq[:, 0 : 2 * P], ws[:, 0 : 2 * P], wg[:, 0:HALF])
+        vector_sign_1(wtmp[:, 0:HALF], wg[:, 0:HALF])
+        nc.scalar.activation(out=swg[:, HALF:], in_=wg[:, HALF:], func=ACT.Sign)
+        quantise_s(0)
+        vector_sign_2(swg[:, 0:HALF], wtmp[:, 0:HALF])
+        quantise(wq[:, 2 * P :], ws[:, 2 * P :], wg[:, HALF:])
+        regroup(1)
+        scalar_sign(1)
+        quantise(swq[:, 0 : 2 * P], sws[:, 0 : 2 * P], swg[:, 0:HALF])
+        quantise(swq[:, 2 * P :], sws[:, 2 * P :], swg[:, HALF:])
+
+        acc = {}
+
+        def pass_sign_x(c, ob, start, stop):
+            cols = slice(ob * P, (ob + 1) * P)
+            nc.tensor.matmul_mx(
+                out=acc[(c, ob)][:],
+                lhsT=wq[:, cols].bitcast(FP8X4),
+                lhsT_scale=ws[:, cols],
+                rhs=sq[c][:].bitcast(FP8X4),
+                rhs_scale=ss[c][:],
+                start=start,
+                stop=stop,
+            )
+
+        def pass_sign_w(c, ob, start, stop):
+            cols = slice(ob * P, (ob + 1) * P)
+            nc.tensor.matmul_mx(
+                out=acc[(c, ob)][:],
+                lhsT=swq[:, cols].bitcast(FP8X4),
+                lhsT_scale=sws[:, cols],
+                rhs=xq[c][:].bitcast(FP8X4),
+                rhs_scale=xs[c][:],
+                start=start,
+                stop=stop,
+            )
+
+        def open_banks(c):
+            for ob in range(BLOCKS):
+                acc[(c, ob)] = psum.tile([P, N_TILE], F32, tag="bank", name="acc%d_%d" % (c, ob))
+
+        def leave(c, pieces):
+            b, half = divmod(c, 2)
+            dram = out[b].rearrange("(m ob) h w -> m ob (h w)", ob=BLOCKS)[:, :, half * N_TILE : (half + 1) * N_TILE]
+            step = BLOCKS // pieces
+            for ob in range(BLOCKS):
+                if EXIT[c][ob] == "s":
+                    nc.scalar.copy(out=res[c][:, ob, :], in_=acc[(c, ob)][:])
+                else:
+                    nc.vector.tensor_copy(out=res[c][:, ob, :], in_=acc[(c, ob)][:])
+                if (ob + 1) % step == 0:
+                    lo = ob + 1 - step
+                    nc.sync.dma_start(out=dram[:, lo : ob + 1, :], in_=res[c][:, lo : ob + 1, :])
+
+        open_banks(0)
+        for ob in range(BLOCKS):
+            pass_sign_x(0, ob, True, False)
+        for ob in range(BLOCKS):
+            pass_sign_w(0, ob, False, True)
+
+        for c in range(1, CHUNKS):
+            quantise_x(c)
+            sign_1(c)
+            open_banks(c)
+            for ob in range(BLOCKS):
+                pass_sign_w(c, ob, True, False)
+            if c + 1 < CHUNKS:
+                regroup(c + 1)
+                scalar_sign(c + 1)
+            sign_2(c)
+            leave(c - 1, 2)
+            quantise_s(c)
+            for ob in range(BLOCKS):
+                pass_sign_x(c, ob, False, True)
+        leave(CHUNKS - 1, 4)

@@ -1,3 +1,5 @@
+from contextlib import ExitStack
+
 import concourse.mybir as mybir
 from concourse.masks import make_identity
 
@@ -13,15 +15,38 @@ ACT = mybir.ActivationFunctionType
 
 P = 128
 PACK = 4
-N_TILE = 512
-CHUNKS = 4
 BLOCKS = 4
+HW = 1024
 TINY = 2.0 ** -133
 UP_A = 2.0 ** 67
 UP_B = 2.0 ** 66
 
-SCALAR_SIGN_COLS = (512, 128, 128, 96)
-EXIT = ("ssss", "ssss", "ssss", "svsv")
+PIN = True
+WIDTHS = (512, 512, 512, 512,)
+STARTS = (0, 512, 1024, 1536,)
+SCALAR_SIGN_COLS = (512, 256, 192, 192,)
+LOADS = {0: (0,), 1: (1,), 2: (2, 3,)}
+EXIT = ("ssss", "ssss", "ssss", "svsv",)
+STORES = (((0, 1), (1, 2), (2, 4),), ((0, 2), (2, 4),), ((0, 2), (2, 4),), ((0, 1), (1, 2), (2, 3), (3, 4),),)
+EXW = ("v", "s",)
+ORDER = (
+    ("L", 0), ("LW",), ("L", 1), ("L", 2), ("RG", 0), ("SG", 0),
+    ("T", 0), ("Qx", 0), ("T", 1), ("EXw", 0), ("Qs", 0), ("EXw", 1),
+    ("I1w", 0), ("Qw", 0), ("SGw", 1), ("I2w", 0), ("B", 0, 0), ("Qw", 1),
+    ("B", 0, 1), ("Qsw", 0), ("RG", 1), ("SG", 1), ("A", 0, 0), ("A", 0, 1),
+    ("B", 0, 2), ("B", 0, 3), ("Qsw", 1), ("EX", 0, 0), ("I1", 1), ("A", 0, 2),
+    ("EX", 0, 1), ("Qx", 1), ("A", 0, 3), ("ST", 0, 0), ("EX", 0, 2), ("I2", 1),
+    ("ST", 0, 1), ("A", 1, 0), ("RG", 2), ("EX", 0, 3), ("A", 1, 1), ("A", 1, 2),
+    ("SG", 2), ("A", 1, 3), ("ST", 0, 2), ("Qs", 1), ("I1", 2), ("B", 1, 0),
+    ("Qx", 2), ("B", 1, 1), ("EX", 1, 0), ("B", 1, 2), ("I2", 2), ("B", 1, 3),
+    ("EX", 1, 1), ("RG", 3), ("A", 2, 0), ("A", 2, 1), ("EX", 1, 2), ("A", 2, 2),
+    ("ST", 1, 0), ("A", 2, 3), ("EX", 1, 3), ("Qs", 2), ("SG", 3), ("I1", 3),
+    ("ST", 1, 1), ("B", 2, 0), ("Qx", 3), ("B", 2, 1), ("EX", 2, 0), ("B", 2, 2),
+    ("I2", 3), ("B", 2, 3), ("EX", 2, 1), ("A", 3, 0), ("Qs", 3), ("A", 3, 1),
+    ("EX", 2, 2), ("A", 3, 2), ("ST", 2, 0), ("A", 3, 3), ("EX", 2, 3), ("B", 3, 0),
+    ("B", 3, 1), ("EX", 3, 0), ("B", 3, 2), ("ST", 2, 1), ("EX", 3, 1), ("B", 3, 3),
+    ("EX", 3, 2), ("ST", 3, 0), ("EX", 3, 3), ("ST", 3, 1), ("ST", 3, 2), ("ST", 3, 3),
+)
 
 
 def by_fours(grouped_ap, rows_ap):
@@ -33,31 +58,34 @@ def by_fours(grouped_ap, rows_ap):
 
 def tile_pointwise_kernel(tc, x, weight, alpha_x, alpha_w, out):
     nc = tc.nc
-    with tc.tile_pool(name="keep", bufs=1) as keep, tc.psum_pool(name="psum", bufs=8) as psum:
-        raw = []
-        w_sb = keep.tile([P, BLOCKS * 512], BF16, name="w_sb")
-        for c in range(CHUNKS):
-            b, half = divmod(c, 2)
-            r = keep.tile([P, PACK, N_TILE], BF16, name="raw%d" % c)
-            raw.append(r)
-            nc.sync.dma_start(
-                out=r[:],
-                in_=x[b].rearrange("(p j) h w -> p j (h w)", j=PACK)[:, :, half * N_TILE : (half + 1) * N_TILE],
-            )
-            if c == 0:
-                nc.sync.dma_start(out=w_sb[:], in_=weight.rearrange("(p ob) c a b -> p (ob c a b)", ob=BLOCKS))
+    chunks = range(len(WIDTHS))
+    with ExitStack() as ctx:
+        keep = ctx.enter_context(tc.tile_pool(name="keep", bufs=1))
+        psum = ctx.enter_context(tc.psum_pool(name="psum", bufs=1))
+        if PIN:
+            ctx.enter_context(tc.manual_schedule())
 
+        w_sb = keep.tile([P, BLOCKS * 512], BF16, name="w_sb")
         ident = keep.tile([P, P], F32, name="ident")
         make_identity(nc, ident[:])
 
-        xg = [keep.tile([P, N_TILE, PACK], BF16, name="xg%d" % c, align_bytes=64) for c in range(CHUNKS)]
-        sg = [keep.tile([P, N_TILE, PACK], BF16, name="sg%d" % c, align_bytes=64) for c in range(CHUNKS)]
-        tmp = [keep.tile([P, N_TILE, PACK], BF16, name="tmp%d" % c, align_bytes=64) for c in range(CHUNKS)]
-        xq = [keep.tile([P, N_TILE], U32, name="xq%d" % c, align_bytes=64) for c in range(CHUNKS)]
-        xs = [keep.tile([P, N_TILE], U8, name="xs%d" % c, align_bytes=64) for c in range(CHUNKS)]
-        sq = [keep.tile([P, N_TILE], U32, name="sq%d" % c, align_bytes=64) for c in range(CHUNKS)]
-        ss = [keep.tile([P, N_TILE], U8, name="ss%d" % c, align_bytes=64) for c in range(CHUNKS)]
-        res = [keep.tile([P, BLOCKS, N_TILE], F32, name="res%d" % c) for c in range(CHUNKS)]
+        raw = {}
+        raw_view = {}
+        for first in LOADS:
+            cols = sum(WIDTHS[c] for c in LOADS[first])
+            raw[first] = keep.tile([P, PACK, cols], BF16, name="raw%d" % first)
+            for c in LOADS[first]:
+                lo = STARTS[c] - STARTS[first]
+                raw_view[c] = raw[first][:, :, lo : lo + WIDTHS[c]]
+
+        xg = [keep.tile([P, WIDTHS[c], PACK], BF16, name="xg%d" % c, align_bytes=64) for c in chunks]
+        sg = [keep.tile([P, WIDTHS[c], PACK], BF16, name="sg%d" % c, align_bytes=64) for c in chunks]
+        tmp = [keep.tile([P, WIDTHS[c], PACK], BF16, name="tmp%d" % c, align_bytes=64) for c in chunks]
+        xq = [keep.tile([P, WIDTHS[c]], U32, name="xq%d" % c, align_bytes=64) for c in chunks]
+        xs = [keep.tile([P, WIDTHS[c]], U8, name="xs%d" % c, align_bytes=64) for c in chunks]
+        sq = [keep.tile([P, WIDTHS[c]], U32, name="sq%d" % c, align_bytes=64) for c in chunks]
+        ss = [keep.tile([P, WIDTHS[c]], U8, name="ss%d" % c, align_bytes=64) for c in chunks]
+        res = [keep.tile([P, BLOCKS, WIDTHS[c]], F32, name="res%d" % c) for c in chunks]
 
         wg = keep.tile([P, BLOCKS * P * PACK], BF16, name="wg", align_bytes=64)
         swg = keep.tile([P, BLOCKS * P * PACK], BF16, name="swg", align_bytes=64)
@@ -67,132 +95,149 @@ def tile_pointwise_kernel(tc, x, weight, alpha_x, alpha_w, out):
         swq = keep.tile([P, BLOCKS * P], U32, name="swq", align_bytes=64)
         sws = keep.tile([P, BLOCKS * P], U8, name="sws", align_bytes=64)
 
+        w_words = w_sb[:].bitcast(F32).rearrange("p (ob q u) -> p ob q u", ob=BLOCKS, u=2)
+        wg_words = wg[:].bitcast(F32).rearrange("p (ob m u) -> p ob m u", ob=BLOCKS, u=2)
+        half = 2 * P * PACK
+        state = {"bank": 0}
+        wt = {}
+        acc = {}
+        opened = set()
+
+        def new_bank(shape, name):
+            k = state["bank"] % 8
+            state["bank"] = state["bank"] + 1
+            return psum.tile(shape, F32, tag="bank%d" % k, name=name)
+
         def quantise(codes, scales, values):
             nc.vector.quantize_mx(out=codes.bitcast(FP8X4), scales=scales, in_=values)
 
-        def vector_sign_1(dst, src):
+        def clamp(dst, src):
             nc.vector.tensor_scalar(out=dst, in0=src, scalar1=-TINY, scalar2=TINY, op0=ALU.max, op1=ALU.min)
 
-        def vector_sign_2(dst, src):
+        def blow_up(dst, src):
             nc.vector.tensor_scalar(out=dst, in0=src, scalar1=UP_A, scalar2=UP_B, op0=ALU.mult, op1=ALU.mult)
-
-        def regroup(c):
-            dst, src = by_fours(xg[c][:], raw[c][:])
-            nc.vector.tensor_copy(out=dst, in_=src)
-
-        def scalar_sign(c):
-            n = SCALAR_SIGN_COLS[c]
-            if n:
-                dst, src = by_fours(sg[c][:, :n, :], raw[c][:, :, :n])
-                nc.scalar.activation(out=dst, in_=src, func=ACT.Sign)
 
         def flat(t, c, lo):
             return t[c][:, lo:, :].rearrange("p w j -> p (w j)")
 
-        def sign_1(c):
-            n = SCALAR_SIGN_COLS[c]
-            if n < N_TILE:
-                vector_sign_1(flat(tmp, c, n), flat(xg, c, n))
+        def op_load(first):
+            b, lo = divmod(STARTS[first], HW)
+            cols = sum(WIDTHS[c] for c in LOADS[first])
+            nc.sync.dma_start(
+                out=raw[first][:],
+                in_=x[b].rearrange("(p j) h w -> p j (h w)", j=PACK)[:, :, lo : lo + cols],
+            )
 
-        def sign_2(c):
-            n = SCALAR_SIGN_COLS[c]
-            if n < N_TILE:
-                vector_sign_2(flat(sg, c, n), flat(tmp, c, n))
+        def op_load_w():
+            nc.sync.dma_start(out=w_sb[:], in_=weight.rearrange("(p ob) c a b -> p (ob c a b)", ob=BLOCKS))
 
-        def quantise_x(c):
-            quantise(xq[c][:], xs[c][:], flat(xg, c, 0))
-
-        def quantise_s(c):
-            quantise(sq[c][:], ss[c][:], flat(sg, c, 0))
-
-        w_words = w_sb[:].bitcast(F32).rearrange("p (ob q u) -> p ob q u", ob=BLOCKS, u=2)
-        wg_words = wg[:].bitcast(F32).rearrange("p (ob m u) -> p ob m u", ob=BLOCKS, u=2)
-        HALF = 2 * P * PACK
-
-        regroup(0)
-        scalar_sign(0)
-        wt = []
-        for pair in range(2):
-            pt = psum.tile([P, 2, 2, P], F32, tag="bank", name="wt%d" % pair)
-            wt.append(pt)
+        def op_t(pair):
+            wt[pair] = new_bank([P, 2, 2, P], "wt%d" % pair)
             for i in range(2):
                 for u in range(2):
-                    nc.tensor.transpose(pt[:, i, u, :], w_words[:, 2 * pair + i, :, u], ident[:])
-        quantise_x(0)
-        nc.vector.tensor_copy(out=wg_words[:, 0:2], in_=wt[0][:].rearrange("p i u m -> p i m u"))
-        nc.scalar.copy(out=wg_words[:, 2:4], in_=wt[1][:].rearrange("p i u m -> p i m u"))
-        quantise(wq[:, 0 : 2 * P], ws[:, 0 : 2 * P], wg[:, 0:HALF])
-        vector_sign_1(wtmp[:, 0:HALF], wg[:, 0:HALF])
-        nc.scalar.activation(out=swg[:, HALF:], in_=wg[:, HALF:], func=ACT.Sign)
-        quantise_s(0)
-        vector_sign_2(swg[:, 0:HALF], wtmp[:, 0:HALF])
-        quantise(wq[:, 2 * P :], ws[:, 2 * P :], wg[:, HALF:])
-        regroup(1)
-        scalar_sign(1)
-        quantise(swq[:, 0 : 2 * P], sws[:, 0 : 2 * P], swg[:, 0:HALF])
-        quantise(swq[:, 2 * P :], sws[:, 2 * P :], swg[:, HALF:])
+                    nc.tensor.transpose(wt[pair][:, i, u, :], w_words[:, 2 * pair + i, :, u], ident[:])
 
-        acc = {}
+        def op_exw(pair):
+            dst = wg_words[:, 2 * pair : 2 * pair + 2]
+            src = wt[pair][:].rearrange("p i u m -> p i m u")
+            if EXW[pair] == "v":
+                nc.vector.tensor_copy(out=dst, in_=src)
+            else:
+                nc.scalar.copy(out=dst, in_=src)
 
-        def pass_sign_x(c, ob, start, stop):
+        def wcols(pair):
+            return slice(pair * 2 * P, (pair + 1) * 2 * P)
+
+        def wvals(pair):
+            return slice(pair * half, (pair + 1) * half)
+
+        def op_qw(pair):
+            quantise(wq[:, wcols(pair)], ws[:, wcols(pair)], wg[:, wvals(pair)])
+
+        def op_i1w(pair):
+            clamp(wtmp[:, wvals(pair)], wg[:, wvals(pair)])
+
+        def op_i2w(pair):
+            blow_up(swg[:, wvals(pair)], wtmp[:, wvals(pair)])
+
+        def op_sgw(pair):
+            nc.scalar.activation(out=swg[:, wvals(pair)], in_=wg[:, wvals(pair)], func=ACT.Sign)
+
+        def op_qsw(pair):
+            quantise(swq[:, wcols(pair)], sws[:, wcols(pair)], swg[:, wvals(pair)])
+
+        def op_rg(c):
+            dst, src = by_fours(xg[c][:], raw_view[c])
+            nc.vector.tensor_copy(out=dst, in_=src)
+
+        def op_sg(c):
+            n = SCALAR_SIGN_COLS[c]
+            dst, src = by_fours(sg[c][:, :n, :], raw_view[c][:, :, :n])
+            nc.scalar.activation(out=dst, in_=src, func=ACT.Sign)
+
+        def op_i1(c):
+            n = SCALAR_SIGN_COLS[c]
+            clamp(flat(tmp, c, n), flat(xg, c, n))
+
+        def op_i2(c):
+            n = SCALAR_SIGN_COLS[c]
+            blow_up(flat(sg, c, n), flat(tmp, c, n))
+
+        def op_qx(c):
+            quantise(xq[c][:], xs[c][:], flat(xg, c, 0))
+
+        def op_qs(c):
+            quantise(sq[c][:], ss[c][:], flat(sg, c, 0))
+
+        def target(c, ob):
+            per_bank = 512 // WIDTHS[c]
+            g = ob // per_bank
+            if (c, g) not in acc:
+                acc[(c, g)] = new_bank([P, per_bank, WIDTHS[c]], "acc%d_%d" % (c, g))
+            return acc[(c, g)][:, ob % per_bank, :]
+
+        def mx_pass(c, ob, w_codes, w_scales, x_codes, x_scales):
             cols = slice(ob * P, (ob + 1) * P)
+            first = (c, ob) not in opened
+            opened.add((c, ob))
             nc.tensor.matmul_mx(
-                out=acc[(c, ob)][:],
-                lhsT=wq[:, cols].bitcast(FP8X4),
-                lhsT_scale=ws[:, cols],
-                rhs=sq[c][:].bitcast(FP8X4),
-                rhs_scale=ss[c][:],
-                start=start,
-                stop=stop,
+                out=target(c, ob),
+                lhsT=w_codes[:, cols].bitcast(FP8X4),
+                lhsT_scale=w_scales[:, cols],
+                rhs=x_codes[c][:].bitcast(FP8X4),
+                rhs_scale=x_scales[c][:],
+                start=first,
+                stop=not first,
             )
 
-        def pass_sign_w(c, ob, start, stop):
-            cols = slice(ob * P, (ob + 1) * P)
-            nc.tensor.matmul_mx(
-                out=acc[(c, ob)][:],
-                lhsT=swq[:, cols].bitcast(FP8X4),
-                lhsT_scale=sws[:, cols],
-                rhs=xq[c][:].bitcast(FP8X4),
-                rhs_scale=xs[c][:],
-                start=start,
-                stop=stop,
+        def op_a(c, ob):
+            mx_pass(c, ob, swq, sws, xq, xs)
+
+        def op_b(c, ob):
+            mx_pass(c, ob, wq, ws, sq, ss)
+
+        def op_ex(c, g):
+            per_bank = 512 // WIDTHS[c]
+            dst = res[c][:, g * per_bank : (g + 1) * per_bank, :]
+            if EXIT[c][g] == "s":
+                nc.scalar.copy(out=dst, in_=acc[(c, g)][:])
+            else:
+                nc.vector.tensor_copy(out=dst, in_=acc[(c, g)][:])
+
+        def op_st(c, i):
+            per_bank = 512 // WIDTHS[c]
+            g0, g1 = STORES[c][i]
+            b, lo = divmod(STARTS[c], HW)
+            dram = out[b].rearrange("(m ob) h w -> m ob (h w)", ob=BLOCKS)[:, :, lo : lo + WIDTHS[c]]
+            nc.sync.dma_start(
+                out=dram[:, g0 * per_bank : g1 * per_bank, :],
+                in_=res[c][:, g0 * per_bank : g1 * per_bank, :],
             )
 
-        def open_banks(c):
-            for ob in range(BLOCKS):
-                acc[(c, ob)] = psum.tile([P, N_TILE], F32, tag="bank", name="acc%d_%d" % (c, ob))
-
-        def leave(c, pieces):
-            b, half = divmod(c, 2)
-            dram = out[b].rearrange("(m ob) h w -> m ob (h w)", ob=BLOCKS)[:, :, half * N_TILE : (half + 1) * N_TILE]
-            step = BLOCKS // pieces
-            for ob in range(BLOCKS):
-                if EXIT[c][ob] == "s":
-                    nc.scalar.copy(out=res[c][:, ob, :], in_=acc[(c, ob)][:])
-                else:
-                    nc.vector.tensor_copy(out=res[c][:, ob, :], in_=acc[(c, ob)][:])
-                if (ob + 1) % step == 0:
-                    lo = ob + 1 - step
-                    nc.sync.dma_start(out=dram[:, lo : ob + 1, :], in_=res[c][:, lo : ob + 1, :])
-
-        open_banks(0)
-        for ob in range(BLOCKS):
-            pass_sign_x(0, ob, True, False)
-        for ob in range(BLOCKS):
-            pass_sign_w(0, ob, False, True)
-
-        for c in range(1, CHUNKS):
-            quantise_x(c)
-            sign_1(c)
-            open_banks(c)
-            for ob in range(BLOCKS):
-                pass_sign_w(c, ob, True, False)
-            if c + 1 < CHUNKS:
-                regroup(c + 1)
-                scalar_sign(c + 1)
-            sign_2(c)
-            leave(c - 1, 2)
-            quantise_s(c)
-            for ob in range(BLOCKS):
-                pass_sign_x(c, ob, False, True)
-        leave(CHUNKS - 1, 4)
+        ops = {
+            "L": op_load, "LW": op_load_w, "T": op_t, "EXw": op_exw, "Qw": op_qw, "I1w": op_i1w, "I2w": op_i2w,
+            "SGw": op_sgw, "Qsw": op_qsw, "RG": op_rg, "SG": op_sg, "I1": op_i1, "I2": op_i2, "Qx": op_qx,
+            "Qs": op_qs, "A": op_a, "B": op_b, "EX": op_ex, "ST": op_st,
+        }
+        for step in ORDER:
+            ops[step[0]](*step[1:])

@@ -27,7 +27,7 @@ STARTS = (0, 512, 1024, 1536,)
 SCALAR_SIGN_COLS = (512, 256, 192, 192,)
 LOADS = {0: (0,), 1: (1,), 2: (2, 3,)}
 EXIT = ("ssss", "ssss", "ssss", "svsv",)
-STORES = (((0, 1), (1, 2), (2, 4),), ((0, 2), (2, 4),), ((0, 2), (2, 4),), ((0, 1), (1, 2), (2, 3), (3, 4),),)
+STORES = (((0, 1), (1, 2), (2, 3), (3, 4),), ((0, 1), (1, 2), (2, 3), (3, 4),), ((0, 1), (1, 2), (2, 3), (3, 4),), ((0, 1), (1, 2), (2, 3), (3, 4),),)
 EXW = ("v", "s",)
 ORDER = (
     ("L", 0), ("LW",), ("L", 1), ("L", 2), ("RG", 0), ("SG", 0),
@@ -36,16 +36,17 @@ ORDER = (
     ("B", 0, 1), ("Qsw", 0), ("RG", 1), ("SG", 1), ("A", 0, 0), ("A", 0, 1),
     ("B", 0, 2), ("B", 0, 3), ("Qsw", 1), ("EX", 0, 0), ("I1", 1), ("A", 0, 2),
     ("EX", 0, 1), ("Qx", 1), ("A", 0, 3), ("ST", 0, 0), ("EX", 0, 2), ("I2", 1),
-    ("ST", 0, 1), ("A", 1, 0), ("RG", 2), ("EX", 0, 3), ("A", 1, 1), ("A", 1, 2),
-    ("SG", 2), ("A", 1, 3), ("ST", 0, 2), ("Qs", 1), ("I1", 2), ("B", 1, 0),
-    ("Qx", 2), ("B", 1, 1), ("EX", 1, 0), ("B", 1, 2), ("I2", 2), ("B", 1, 3),
-    ("EX", 1, 1), ("RG", 3), ("A", 2, 0), ("A", 2, 1), ("EX", 1, 2), ("A", 2, 2),
-    ("ST", 1, 0), ("A", 2, 3), ("EX", 1, 3), ("Qs", 2), ("SG", 3), ("I1", 3),
-    ("ST", 1, 1), ("B", 2, 0), ("Qx", 3), ("B", 2, 1), ("EX", 2, 0), ("B", 2, 2),
-    ("I2", 3), ("B", 2, 3), ("EX", 2, 1), ("A", 3, 0), ("Qs", 3), ("A", 3, 1),
-    ("EX", 2, 2), ("A", 3, 2), ("ST", 2, 0), ("A", 3, 3), ("EX", 2, 3), ("B", 3, 0),
-    ("B", 3, 1), ("EX", 3, 0), ("B", 3, 2), ("ST", 2, 1), ("EX", 3, 1), ("B", 3, 3),
-    ("EX", 3, 2), ("ST", 3, 0), ("EX", 3, 3), ("ST", 3, 1), ("ST", 3, 2), ("ST", 3, 3),
+    ("ST", 0, 1), ("A", 1, 0), ("RG", 2), ("EX", 0, 3), ("A", 1, 1), ("ST", 0, 2),
+    ("A", 1, 2), ("SG", 2), ("A", 1, 3), ("ST", 0, 3), ("Qs", 1), ("I1", 2),
+    ("B", 1, 0), ("Qx", 2), ("B", 1, 1), ("EX", 1, 0), ("B", 1, 2), ("I2", 2),
+    ("B", 1, 3), ("EX", 1, 1), ("RG", 3), ("A", 2, 0), ("ST", 1, 0), ("A", 2, 1),
+    ("EX", 1, 2), ("A", 2, 2), ("ST", 1, 1), ("A", 2, 3), ("EX", 1, 3), ("Qs", 2),
+    ("ST", 1, 2), ("SG", 3), ("I1", 3), ("ST", 1, 3), ("B", 2, 0), ("Qx", 3),
+    ("B", 2, 1), ("EX", 2, 0), ("B", 2, 2), ("I2", 3), ("B", 2, 3), ("EX", 2, 1),
+    ("A", 3, 0), ("ST", 2, 0), ("Qs", 3), ("A", 3, 1), ("EX", 2, 2), ("A", 3, 2),
+    ("ST", 2, 1), ("A", 3, 3), ("EX", 2, 3), ("B", 3, 0), ("ST", 2, 2), ("B", 3, 1),
+    ("EX", 3, 0), ("B", 3, 2), ("ST", 2, 3), ("EX", 3, 1), ("B", 3, 3), ("EX", 3, 2),
+    ("ST", 3, 0), ("EX", 3, 3), ("ST", 3, 1), ("ST", 3, 2), ("ST", 3, 3),
 )
 
 
@@ -98,15 +99,15 @@ def tile_pointwise_kernel(tc, x, weight, alpha_x, alpha_w, out):
         w_words = w_sb[:].bitcast(F32).rearrange("p (ob q u) -> p ob q u", ob=BLOCKS, u=2)
         wg_words = wg[:].bitcast(F32).rearrange("p (ob m u) -> p ob m u", ob=BLOCKS, u=2)
         half = 2 * P * PACK
-        state = {"bank": 0}
         wt = {}
         acc = {}
         opened = set()
 
-        def new_bank(shape, name):
-            k = state["bank"] % 8
-            state["bank"] = state["bank"] + 1
-            return psum.tile(shape, F32, tag="bank%d" % k, name=name)
+        def new_bank(shape, name, k):
+            return psum.tile(shape, F32, tag="bank%d" % (k % 8), name=name)
+
+        def banks_before(c):
+            return 2 + sum(BLOCKS * WIDTHS[i] // 512 for i in range(c))
 
         def quantise(codes, scales, values):
             nc.vector.quantize_mx(out=codes.bitcast(FP8X4), scales=scales, in_=values)
@@ -132,7 +133,7 @@ def tile_pointwise_kernel(tc, x, weight, alpha_x, alpha_w, out):
             nc.sync.dma_start(out=w_sb[:], in_=weight.rearrange("(p ob) c a b -> p (ob c a b)", ob=BLOCKS))
 
         def op_t(pair):
-            wt[pair] = new_bank([P, 2, 2, P], "wt%d" % pair)
+            wt[pair] = new_bank([P, 2, 2, P], "wt%d" % pair, pair)
             for i in range(2):
                 for u in range(2):
                     nc.tensor.transpose(wt[pair][:, i, u, :], w_words[:, 2 * pair + i, :, u], ident[:])
@@ -193,7 +194,7 @@ def tile_pointwise_kernel(tc, x, weight, alpha_x, alpha_w, out):
             per_bank = 512 // WIDTHS[c]
             g = ob // per_bank
             if (c, g) not in acc:
-                acc[(c, g)] = new_bank([P, per_bank, WIDTHS[c]], "acc%d_%d" % (c, g))
+                acc[(c, g)] = new_bank([P, per_bank, WIDTHS[c]], "acc%d_%d" % (c, g), banks_before(c) + g)
             return acc[(c, g)][:, ob % per_bank, :]
 
         def mx_pass(c, ob, w_codes, w_scales, x_codes, x_scales):

@@ -15,39 +15,16 @@ ACT = mybir.ActivationFunctionType
 
 P = 128
 PACK = 4
-BLOCKS = 4
+OBS = 4
 HW = 1024
+N = 512
+CHUNKS = 4
 TINY = 2.0 ** -133
 UP_A = 2.0 ** 67
 UP_B = 2.0 ** 66
 
-PIN = True
-WIDTHS = (512, 512, 512, 512,)
-STARTS = (0, 512, 1024, 1536,)
-SCALAR_SIGN_COLS = (512, 256, 192, 192,)
-LOADS = {0: (0,), 1: (1,), 2: (2, 3,)}
-EXIT = ("ssss", "ssss", "ssss", "svsv",)
-STORES = (((0, 1), (1, 2), (2, 3), (3, 4),), ((0, 1), (1, 2), (2, 3), (3, 4),), ((0, 1), (1, 2), (2, 3), (3, 4),), ((0, 1), (1, 2), (2, 3), (3, 4),),)
-EXW = ("v", "s",)
-ORDER = (
-    ("L", 0), ("LW",), ("L", 1), ("L", 2), ("RG", 0), ("SG", 0),
-    ("T", 0), ("Qx", 0), ("T", 1), ("EXw", 0), ("Qs", 0), ("EXw", 1),
-    ("I1w", 0), ("Qw", 0), ("SGw", 1), ("I2w", 0), ("B", 0, 0), ("Qw", 1),
-    ("B", 0, 1), ("Qsw", 0), ("RG", 1), ("SG", 1), ("A", 0, 0), ("A", 0, 1),
-    ("B", 0, 2), ("B", 0, 3), ("Qsw", 1), ("EX", 0, 0), ("I1", 1), ("A", 0, 2),
-    ("EX", 0, 1), ("Qx", 1), ("A", 0, 3), ("ST", 0, 0), ("EX", 0, 2), ("I2", 1),
-    ("ST", 0, 1), ("A", 1, 0), ("RG", 2), ("EX", 0, 3), ("A", 1, 1), ("ST", 0, 2),
-    ("A", 1, 2), ("SG", 2), ("A", 1, 3), ("ST", 0, 3), ("Qs", 1), ("I1", 2),
-    ("B", 1, 0), ("Qx", 2), ("B", 1, 1), ("EX", 1, 0), ("B", 1, 2), ("I2", 2),
-    ("B", 1, 3), ("EX", 1, 1), ("RG", 3), ("A", 2, 0), ("ST", 1, 0), ("A", 2, 1),
-    ("EX", 1, 2), ("A", 2, 2), ("ST", 1, 1), ("A", 2, 3), ("EX", 1, 3), ("Qs", 2),
-    ("ST", 1, 2), ("SG", 3), ("I1", 3), ("ST", 1, 3), ("B", 2, 0), ("Qx", 3),
-    ("B", 2, 1), ("EX", 2, 0), ("B", 2, 2), ("I2", 3), ("B", 2, 3), ("EX", 2, 1),
-    ("A", 3, 0), ("ST", 2, 0), ("Qs", 3), ("A", 3, 1), ("EX", 2, 2), ("A", 3, 2),
-    ("ST", 2, 1), ("A", 3, 3), ("EX", 2, 3), ("B", 3, 0), ("ST", 2, 2), ("B", 3, 1),
-    ("EX", 3, 0), ("B", 3, 2), ("ST", 2, 3), ("EX", 3, 1), ("B", 3, 3), ("EX", 3, 2),
-    ("ST", 3, 0), ("EX", 3, 3), ("ST", 3, 1), ("ST", 3, 2), ("ST", 3, 3),
-)
+SCALAR_SIGN_COLS = (512, 384, 320, 128)
+HEAD = 256
 
 
 def by_fours(grouped_ap, rows_ap):
@@ -59,55 +36,66 @@ def by_fours(grouped_ap, rows_ap):
 
 def tile_pointwise_kernel(tc, x, weight, alpha_x, alpha_w, out):
     nc = tc.nc
-    chunks = range(len(WIDTHS))
     with ExitStack() as ctx:
         keep = ctx.enter_context(tc.tile_pool(name="keep", bufs=1))
         psum = ctx.enter_context(tc.psum_pool(name="psum", bufs=1))
-        if PIN:
-            ctx.enter_context(tc.manual_schedule())
+        ctx.enter_context(tc.manual_schedule())
 
-        w_sb = keep.tile([P, BLOCKS * 512], BF16, name="w_sb")
         ident = keep.tile([P, P], F32, name="ident")
         make_identity(nc, ident[:])
 
+        pieces = ((0, 0, HEAD), (0, HEAD, N - HEAD), (1, 0, N), (2, 0, 2 * N))
         raw = {}
-        raw_view = {}
-        for first in LOADS:
-            cols = sum(WIDTHS[c] for c in LOADS[first])
-            raw[first] = keep.tile([P, PACK, cols], BF16, name="raw%d" % first)
-            for c in LOADS[first]:
-                lo = STARTS[c] - STARTS[first]
-                raw_view[c] = raw[first][:, :, lo : lo + WIDTHS[c]]
+        w_sb = {}
 
-        xg = [keep.tile([P, WIDTHS[c], PACK], BF16, name="xg%d" % c, align_bytes=64) for c in chunks]
-        sg = [keep.tile([P, WIDTHS[c], PACK], BF16, name="sg%d" % c, align_bytes=64) for c in chunks]
-        tmp = [keep.tile([P, WIDTHS[c], PACK], BF16, name="tmp%d" % c, align_bytes=64) for c in chunks]
-        xq = [keep.tile([P, WIDTHS[c]], U32, name="xq%d" % c, align_bytes=64) for c in chunks]
-        xs = [keep.tile([P, WIDTHS[c]], U8, name="xs%d" % c, align_bytes=64) for c in chunks]
-        sq = [keep.tile([P, WIDTHS[c]], U32, name="sq%d" % c, align_bytes=64) for c in chunks]
-        ss = [keep.tile([P, WIDTHS[c]], U8, name="ss%d" % c, align_bytes=64) for c in chunks]
-        res = [keep.tile([P, BLOCKS, WIDTHS[c]], F32, name="res%d" % c) for c in chunks]
+        def load_x(i):
+            c, lo, cols = pieces[i]
+            b, first = divmod(c * N + lo, HW)
+            raw[i] = keep.tile([P, PACK, cols], BF16, name="raw%d" % i)
+            nc.sync.dma_start(
+                out=raw[i][:],
+                in_=x[b].rearrange("(p j) h w -> p j (h w)", j=PACK)[:, :, first : first + cols],
+            )
 
-        wg = keep.tile([P, BLOCKS * P * PACK], BF16, name="wg", align_bytes=64)
-        swg = keep.tile([P, BLOCKS * P * PACK], BF16, name="swg", align_bytes=64)
-        wtmp = keep.tile([P, BLOCKS * P * PACK], BF16, name="wtmp", align_bytes=64)
-        wq = keep.tile([P, BLOCKS * P], U32, name="wq", align_bytes=64)
-        ws = keep.tile([P, BLOCKS * P], U8, name="ws", align_bytes=64)
-        swq = keep.tile([P, BLOCKS * P], U32, name="swq", align_bytes=64)
-        sws = keep.tile([P, BLOCKS * P], U8, name="sws", align_bytes=64)
+        def load_w(pair):
+            w_sb[pair] = keep.tile([P, 2, 512], BF16, name="w_sb%d" % pair)
+            nc.sync.dma_start(
+                out=w_sb[pair][:],
+                in_=weight.rearrange("(p ob) c a b -> p ob (c a b)", ob=OBS)[:, 2 * pair : 2 * pair + 2, :],
+            )
 
-        w_words = w_sb[:].bitcast(F32).rearrange("p (ob q u) -> p ob q u", ob=BLOCKS, u=2)
-        wg_words = wg[:].bitcast(F32).rearrange("p (ob m u) -> p ob m u", ob=BLOCKS, u=2)
-        half = 2 * P * PACK
+        load_x(0)
+        load_x(1)
+        load_w(0)
+        load_w(1)
+        load_x(2)
+        load_x(3)
+
+        chunks = range(CHUNKS)
+        xg = [keep.tile([P, N, PACK], BF16, name="xg%d" % c, align_bytes=64) for c in chunks]
+        sg = [keep.tile([P, N, PACK], BF16, name="sg%d" % c, align_bytes=64) for c in chunks]
+        tmp = [keep.tile([P, N, PACK], BF16, name="tmp%d" % c, align_bytes=64) for c in chunks]
+        xq = [keep.tile([P, N], U32, name="xq%d" % c, align_bytes=64) for c in chunks]
+        xs = [keep.tile([P, N], U8, name="xs%d" % c, align_bytes=64) for c in chunks]
+        sq = [keep.tile([P, N], U32, name="sq%d" % c, align_bytes=64) for c in chunks]
+        ss = [keep.tile([P, N], U8, name="ss%d" % c, align_bytes=64) for c in chunks]
+        res = [keep.tile([P, OBS, N], F32, name="res%d" % c) for c in chunks]
+
+        wg = keep.tile([P, OBS * P * PACK], BF16, name="wg", align_bytes=64)
+        swg = keep.tile([P, OBS * P * PACK], BF16, name="swg", align_bytes=64)
+        wtmp = keep.tile([P, OBS * P * PACK], BF16, name="wtmp", align_bytes=64)
+        wq = keep.tile([P, OBS * P], U32, name="wq", align_bytes=64)
+        ws = keep.tile([P, OBS * P], U8, name="ws", align_bytes=64)
+        swq = keep.tile([P, OBS * P], U32, name="swq", align_bytes=64)
+        sws = keep.tile([P, OBS * P], U8, name="sws", align_bytes=64)
+        wg_words = wg[:].bitcast(F32).rearrange("p (ob m u) -> p ob m u", ob=OBS, u=2)
+
         wt = {}
         acc = {}
         opened = set()
 
         def new_bank(shape, name, k):
             return psum.tile(shape, F32, tag="bank%d" % (k % 8), name=name)
-
-        def banks_before(c):
-            return 2 + sum(BLOCKS * WIDTHS[i] // 512 for i in range(c))
 
         def quantise(codes, scales, values):
             nc.vector.quantize_mx(out=codes.bitcast(FP8X4), scales=scales, in_=values)
@@ -121,88 +109,64 @@ def tile_pointwise_kernel(tc, x, weight, alpha_x, alpha_w, out):
         def flat(t, c, lo):
             return t[c][:, lo:, :].rearrange("p w j -> p (w j)")
 
-        def op_load(first):
-            b, lo = divmod(STARTS[first], HW)
-            cols = sum(WIDTHS[c] for c in LOADS[first])
-            nc.sync.dma_start(
-                out=raw[first][:],
-                in_=x[b].rearrange("(p j) h w -> p j (h w)", j=PACK)[:, :, lo : lo + cols],
+        def transpose_w(pair):
+            words = w_sb[pair][:].rearrange("p ob c -> p (ob c)").bitcast(F32).rearrange(
+                "p (ob q u) -> p ob q u", ob=2, u=2
             )
-
-        def op_load_w():
-            nc.sync.dma_start(out=w_sb[:], in_=weight.rearrange("(p ob) c a b -> p (ob c a b)", ob=BLOCKS))
-
-        def op_t(pair):
             wt[pair] = new_bank([P, 2, 2, P], "wt%d" % pair, pair)
             for i in range(2):
                 for u in range(2):
-                    nc.tensor.transpose(wt[pair][:, i, u, :], w_words[:, 2 * pair + i, :, u], ident[:])
+                    nc.tensor.transpose(wt[pair][:, i, u, :], words[:, i, :, u], ident[:])
 
-        def op_exw(pair):
-            dst = wg_words[:, 2 * pair : 2 * pair + 2]
-            src = wt[pair][:].rearrange("p i u m -> p i m u")
-            if EXW[pair] == "v":
-                nc.vector.tensor_copy(out=dst, in_=src)
-            else:
-                nc.scalar.copy(out=dst, in_=src)
+        def exit_w(pair, copy):
+            copy(out=wg_words[:, 2 * pair : 2 * pair + 2], in_=wt[pair][:].rearrange("p i u m -> p i m u"))
 
         def wcols(pair):
             return slice(pair * 2 * P, (pair + 1) * 2 * P)
 
         def wvals(pair):
-            return slice(pair * half, (pair + 1) * half)
+            return slice(pair * 2 * P * PACK, (pair + 1) * 2 * P * PACK)
 
-        def op_qw(pair):
+        def quantise_w(pair):
             quantise(wq[:, wcols(pair)], ws[:, wcols(pair)], wg[:, wvals(pair)])
 
-        def op_i1w(pair):
-            clamp(wtmp[:, wvals(pair)], wg[:, wvals(pair)])
-
-        def op_i2w(pair):
-            blow_up(swg[:, wvals(pair)], wtmp[:, wvals(pair)])
-
-        def op_sgw(pair):
-            nc.scalar.activation(out=swg[:, wvals(pair)], in_=wg[:, wvals(pair)], func=ACT.Sign)
-
-        def op_qsw(pair):
+        def quantise_sw(pair):
             quantise(swq[:, wcols(pair)], sws[:, wcols(pair)], swg[:, wvals(pair)])
 
-        def op_rg(c):
-            dst, src = by_fours(xg[c][:], raw_view[c])
+        def regroup(c, i, dst_lo, src_lo, cols):
+            dst, src = by_fours(xg[c][:, dst_lo : dst_lo + cols, :], raw[i][:, :, src_lo : src_lo + cols])
             nc.vector.tensor_copy(out=dst, in_=src)
 
-        def op_sg(c):
-            n = SCALAR_SIGN_COLS[c]
-            dst, src = by_fours(sg[c][:, :n, :], raw_view[c][:, :, :n])
+        def sign(c, i, dst_lo, src_lo, cols):
+            dst, src = by_fours(sg[c][:, dst_lo : dst_lo + cols, :], raw[i][:, :, src_lo : src_lo + cols])
             nc.scalar.activation(out=dst, in_=src, func=ACT.Sign)
 
-        def op_i1(c):
-            n = SCALAR_SIGN_COLS[c]
-            clamp(flat(tmp, c, n), flat(xg, c, n))
+        def regroup_chunk(c):
+            regroup(c, min(c + 1, 3), 0, N * (c == 3), N)
 
-        def op_i2(c):
-            n = SCALAR_SIGN_COLS[c]
-            blow_up(flat(sg, c, n), flat(tmp, c, n))
+        def sign_chunk(c):
+            sign(c, min(c + 1, 3), 0, N * (c == 3), SCALAR_SIGN_COLS[c])
 
-        def op_qx(c):
+        def clamp_chunk(c):
+            clamp(flat(tmp, c, SCALAR_SIGN_COLS[c]), flat(xg, c, SCALAR_SIGN_COLS[c]))
+
+        def grow_chunk(c):
+            blow_up(flat(sg, c, SCALAR_SIGN_COLS[c]), flat(tmp, c, SCALAR_SIGN_COLS[c]))
+
+        def quantise_x(c):
             quantise(xq[c][:], xs[c][:], flat(xg, c, 0))
 
-        def op_qs(c):
+        def quantise_s(c):
             quantise(sq[c][:], ss[c][:], flat(sg, c, 0))
-
-        def target(c, ob):
-            per_bank = 512 // WIDTHS[c]
-            g = ob // per_bank
-            if (c, g) not in acc:
-                acc[(c, g)] = new_bank([P, per_bank, WIDTHS[c]], "acc%d_%d" % (c, g), banks_before(c) + g)
-            return acc[(c, g)][:, ob % per_bank, :]
 
         def mx_pass(c, ob, w_codes, w_scales, x_codes, x_scales):
             cols = slice(ob * P, (ob + 1) * P)
             first = (c, ob) not in opened
             opened.add((c, ob))
+            if first:
+                acc[(c, ob)] = new_bank([P, N], "acc%d_%d" % (c, ob), 2 + OBS * c + ob)
             nc.tensor.matmul_mx(
-                out=target(c, ob),
+                out=acc[(c, ob)][:],
                 lhsT=w_codes[:, cols].bitcast(FP8X4),
                 lhsT_scale=w_scales[:, cols],
                 rhs=x_codes[c][:].bitcast(FP8X4),
@@ -211,34 +175,69 @@ def tile_pointwise_kernel(tc, x, weight, alpha_x, alpha_w, out):
                 stop=not first,
             )
 
-        def op_a(c, ob):
+        def times_sign_w(c, ob):
             mx_pass(c, ob, swq, sws, xq, xs)
 
-        def op_b(c, ob):
+        def times_w(c, ob):
             mx_pass(c, ob, wq, ws, sq, ss)
 
-        def op_ex(c, g):
-            per_bank = 512 // WIDTHS[c]
-            dst = res[c][:, g * per_bank : (g + 1) * per_bank, :]
-            if EXIT[c][g] == "s":
-                nc.scalar.copy(out=dst, in_=acc[(c, g)][:])
-            else:
-                nc.vector.tensor_copy(out=dst, in_=acc[(c, g)][:])
+        def leave(c, ob, copy):
+            copy(out=res[c][:, ob, :], in_=acc[(c, ob)][:])
+            b, lo = divmod(c * N, HW)
+            dram = out[b].rearrange("(m ob) h w -> m ob (h w)", ob=OBS)[:, :, lo : lo + N]
+            nc.sync.dma_start(out=dram[:, ob : ob + 1, :], in_=res[c][:, ob : ob + 1, :])
 
-        def op_st(c, i):
-            per_bank = 512 // WIDTHS[c]
-            g0, g1 = STORES[c][i]
-            b, lo = divmod(STARTS[c], HW)
-            dram = out[b].rearrange("(m ob) h w -> m ob (h w)", ob=BLOCKS)[:, :, lo : lo + WIDTHS[c]]
-            nc.sync.dma_start(
-                out=dram[:, g0 * per_bank : g1 * per_bank, :],
-                in_=res[c][:, g0 * per_bank : g1 * per_bank, :],
-            )
+        vcopy = nc.vector.tensor_copy
+        scopy = nc.scalar.copy
 
-        ops = {
-            "L": op_load, "LW": op_load_w, "T": op_t, "EXw": op_exw, "Qw": op_qw, "I1w": op_i1w, "I2w": op_i2w,
-            "SGw": op_sgw, "Qsw": op_qsw, "RG": op_rg, "SG": op_sg, "I1": op_i1, "I2": op_i2, "Qx": op_qx,
-            "Qs": op_qs, "A": op_a, "B": op_b, "EX": op_ex, "ST": op_st,
-        }
-        for step in ORDER:
-            ops[step[0]](*step[1:])
+        regroup(0, 0, 0, 0, HEAD)
+        sign(0, 0, 0, 0, HEAD)
+        regroup(0, 1, HEAD, 0, N - HEAD)
+        sign(0, 1, HEAD, 0, N - HEAD)
+        transpose_w(0)
+        transpose_w(1)
+        quantise_x(0)
+        exit_w(0, vcopy)
+        exit_w(1, scopy)
+        quantise_s(0)
+        clamp(wtmp[:, wvals(0)], wg[:, wvals(0)])
+        nc.scalar.activation(out=swg[:, wvals(1)], in_=wg[:, wvals(1)], func=ACT.Sign)
+        quantise_w(0)
+        blow_up(swg[:, wvals(0)], wtmp[:, wvals(0)])
+        times_w(0, 0)
+        times_w(0, 1)
+        quantise_w(1)
+        quantise_sw(0)
+        sign_chunk(1)
+        times_sign_w(0, 0)
+        times_sign_w(0, 1)
+        regroup_chunk(1)
+        times_w(0, 2)
+        times_w(0, 3)
+        quantise_sw(1)
+        times_sign_w(0, 2)
+        times_sign_w(0, 3)
+
+        for c in range(1, CHUNKS):
+            clamp_chunk(c)
+            quantise_x(c)
+            grow_chunk(c)
+            if c == 3:
+                quantise_s(c)
+            leave(c - 1, 0, scopy)
+            leave(c - 1, 1, scopy)
+            leave(c - 1, 2, scopy)
+            if c == 2:
+                sign_chunk(3)
+            leave(c - 1, 3, vcopy if c == 3 else scopy)
+            if c == 1:
+                sign_chunk(2)
+            for ob in range(OBS):
+                times_sign_w(c, ob)
+            if c < 3:
+                regroup_chunk(c + 1)
+                quantise_s(c)
+            for ob in range(OBS):
+                times_w(c, ob)
+        for ob in range(OBS):
+            leave(3, ob, (scopy, vcopy)[ob % 2])

@@ -90,6 +90,9 @@ def tile_pointwise_kernel(tc, x, weight, alpha_x, alpha_w, out):
         sws = keep.tile([P, OBS * P], U8, name="sws", align_bytes=64)
         wg_words = wg[:].bitcast(F32).rearrange("p (ob m u) -> p ob m u", ob=OBS, u=2)
 
+        warm = keep.tile([P, N], BF16, name="warm")
+        nc.vector.memset(warm[:], 0.0)
+
         wt = {}
         acc = {}
         opened = set()
@@ -117,6 +120,12 @@ def tile_pointwise_kernel(tc, x, weight, alpha_x, alpha_w, out):
             for i in range(2):
                 for u in range(2):
                     nc.tensor.transpose(wt[pair][:, i, u, :], words[:, i, :, u], ident[:])
+
+        warm_out = new_bank([P, N], "warm_out", 7)
+
+        def warm_up(passes):
+            for i in range(passes):
+                nc.tensor.matmul(warm_out[:], lhsT=warm[:, :P], rhs=warm[:], start=True, stop=True)
 
         def exit_w(pair, copy):
             copy(out=wg_words[:, 2 * pair : 2 * pair + 2], in_=wt[pair][:].rearrange("p i u m -> p i m u"))
@@ -190,12 +199,14 @@ def tile_pointwise_kernel(tc, x, weight, alpha_x, alpha_w, out):
         vcopy = nc.vector.tensor_copy
         scopy = nc.scalar.copy
 
+        warm_up(6)
         regroup(0, 0, 0, 0, HEAD)
         sign(0, 0, 0, 0, HEAD)
         regroup(0, 1, HEAD, 0, N - HEAD)
         sign(0, 1, HEAD, 0, N - HEAD)
         transpose_w(0)
         transpose_w(1)
+        warm_up(3)
         quantise_x(0)
         exit_w(0, vcopy)
         exit_w(1, scopy)

@@ -25,12 +25,13 @@ UP_B = 2.0 ** 66
 
 SCALAR_SIGN_COLS = (512, 384, 320, 128)
 HEAD = 256
+RUN = 8
 
 
 def by_fours(grouped_ap, rows_ap):
     return (
-        grouped_ap.rearrange("p (c i) t -> p c t i", i=4),
-        rows_ap.rearrange("p t (c i) -> p c t i", i=4),
+        grouped_ap.rearrange("p (c i) t -> p c t i", i=RUN),
+        rows_ap.rearrange("p t (c i) -> p c t i", i=RUN),
     )
 
 

@@ -166,6 +166,9 @@ def tile_pointwise_kernel(tc, x, weight, alpha_x, alpha_w, out):
         def quantise_x(c):
             quantise(xq[c][:], xs[c][:], flat(xg, c, 0))
 
+        def quantise_x_part(c, lo, hi):
+            quantise(xq[c][:, lo:hi], xs[c][:, lo:hi], xg[c][:, lo:hi, :].rearrange("p w j -> p (w j)"))
+
         def quantise_s(c):
             quantise(sq[c][:], ss[c][:], flat(sg, c, 0))
 
@@ -232,9 +235,13 @@ def tile_pointwise_kernel(tc, x, weight, alpha_x, alpha_w, out):
 
         for c in range(1, CHUNKS):
             clamp_chunk(c)
-            quantise_x(c)
-            grow_chunk(c)
-            if c == 3:
+            if c < 3:
+                quantise_x(c)
+                grow_chunk(c)
+            else:
+                quantise_x_part(c, 0, HEAD)
+                grow_chunk(c)
+                quantise_x_part(c, HEAD, N)
                 quantise_s(c)
             leave(c - 1, 0, scopy)
             leave(c - 1, 1, scopy)
@@ -244,12 +251,21 @@ def tile_pointwise_kernel(tc, x, weight, alpha_x, alpha_w, out):
             leave(c - 1, 3, vcopy if c == 3 else scopy)
             if c == 1:
                 sign_chunk(2)
-            for ob in range(OBS):
-                times_sign_w(c, ob)
             if c < 3:
+                for ob in range(OBS):
+                    times_sign_w(c, ob)
                 regroup_chunk(c + 1)
                 quantise_s(c)
-            for ob in range(OBS):
-                times_w(c, ob)
+                for ob in range(OBS):
+                    times_w(c, ob)
+            else:
+                times_sign_w(3, 0)
+                times_sign_w(3, 1)
+                times_w(3, 0)
+                times_sign_w(3, 2)
+                times_w(3, 1)
+                times_sign_w(3, 3)
+                times_w(3, 2)
+                times_w(3, 3)
         for ob in range(OBS):
             leave(3, ob, (scopy, vcopy)[ob % 2])

@@ -23,7 +23,7 @@ TINY = 2.0 ** -133
 UP_A = 2.0 ** 67
 UP_B = 2.0 ** 66
 
-SCALAR_SIGN_COLS = (512, 384, 320, 128)
+VECTOR_SIGN = ((192, 256), (384, 512), (320, 512), (64, 512))
 HEAD = 256
 RUN = 8
 
@@ -110,8 +110,8 @@ def tile_pointwise_kernel(tc, x, weight, alpha_x, alpha_w, out):
         def blow_up(dst, src):
             nc.vector.tensor_scalar(out=dst, in0=src, scalar1=UP_A, scalar2=UP_B, op0=ALU.mult, op1=ALU.mult)
 
-        def flat(t, c, lo):
-            return t[c][:, lo:, :].rearrange("p w j -> p (w j)")
+        def flat(t, c, lo=0, hi=N):
+            return t[c][:, lo:hi, :].rearrange("p w j -> p (w j)")
 
         def transpose_w(pair):
             words = w_sb[pair][:].rearrange("p ob c -> p (ob c)").bitcast(F32).rearrange(
@@ -155,22 +155,22 @@ def tile_pointwise_kernel(tc, x, weight, alpha_x, alpha_w, out):
             regroup(c, min(c + 1, 3), 0, N * (c == 3), N)
 
         def sign_chunk(c):
-            sign(c, min(c + 1, 3), 0, N * (c == 3), SCALAR_SIGN_COLS[c])
+            sign(c, min(c + 1, 3), 0, N * (c == 3), VECTOR_SIGN[c][0])
 
         def clamp_chunk(c):
-            clamp(flat(tmp, c, SCALAR_SIGN_COLS[c]), flat(xg, c, SCALAR_SIGN_COLS[c]))
+            clamp(flat(tmp, c, *VECTOR_SIGN[c]), flat(xg, c, *VECTOR_SIGN[c]))
 
         def grow_chunk(c):
-            blow_up(flat(sg, c, SCALAR_SIGN_COLS[c]), flat(tmp, c, SCALAR_SIGN_COLS[c]))
+            blow_up(flat(sg, c, *VECTOR_SIGN[c]), flat(tmp, c, *VECTOR_SIGN[c]))
 
         def quantise_x(c):
-            quantise(xq[c][:], xs[c][:], flat(xg, c, 0))
+            quantise(xq[c][:], xs[c][:], flat(xg, c))
 
         def quantise_x_part(c, lo, hi):
             quantise(xq[c][:, lo:hi], xs[c][:, lo:hi], xg[c][:, lo:hi, :].rearrange("p w j -> p (w j)"))
 
         def quantise_s(c):
-            quantise(sq[c][:], ss[c][:], flat(sg, c, 0))
+            quantise(sq[c][:], ss[c][:], flat(sg, c))
 
         def mx_pass(c, ob, w_codes, w_scales, x_codes, x_scales):
             cols = slice(ob * P, (ob + 1) * P)
@@ -205,14 +205,16 @@ def tile_pointwise_kernel(tc, x, weight, alpha_x, alpha_w, out):
 
         warm_up(6)
         regroup(0, 0, 0, 0, HEAD)
-        sign(0, 0, 0, 0, HEAD)
+        sign(0, 0, 0, 0, VECTOR_SIGN[0][0])
         regroup(0, 1, HEAD, 0, N - HEAD)
         sign(0, 1, HEAD, 0, N - HEAD)
         transpose_w(0)
         transpose_w(1)
         warm_up(3)
+        clamp_chunk(0)
         quantise_x(0)
-        exit_w(0, vcopy)
+        grow_chunk(0)
+        exit_w(0, scopy)
         exit_w(1, scopy)
         quantise_s(0)
         clamp(wtmp[:, wvals(0)], wg[:, wvals(0)])
@@ -246,11 +248,9 @@ def tile_pointwise_kernel(tc, x, weight, alpha_x, alpha_w, out):
             leave(c - 1, 0, scopy)
             leave(c - 1, 1, scopy)
             leave(c - 1, 2, scopy)
-            if c == 2:
-                sign_chunk(3)
-            leave(c - 1, 3, vcopy if c == 3 else scopy)
-            if c == 1:
-                sign_chunk(2)
+            leave(c - 1, 3, scopy)
+            if c < 3:
+                sign_chunk(c + 1)
             if c < 3:
                 for ob in range(OBS):
                     times_sign_w(c, ob)

@@ -23,7 +23,7 @@ TINY = 2.0 ** -133
 UP_A = 2.0 ** 67
 UP_B = 2.0 ** 66
 
-VECTOR_SIGN = ((192, 256), (384, 512), (320, 512), (64, 512))
+VECTOR_SIGN = ((192, 256), (512, 512), (256, 512), (0, 512))
 HEAD = 256
 RUN = 8
 
@@ -236,10 +236,12 @@ def tile_pointwise_kernel(tc, x, weight, alpha_x, alpha_w, out):
         times_sign_w(0, 3)
 
         for c in range(1, CHUNKS):
-            clamp_chunk(c)
+            if c > 1:
+                clamp_chunk(c)
             if c < 3:
                 quantise_x(c)
-                grow_chunk(c)
+                if c > 1:
+                    grow_chunk(c)
             else:
                 quantise_x_part(c, 0, HEAD)
                 grow_chunk(c)
@@ -249,8 +251,8 @@ def tile_pointwise_kernel(tc, x, weight, alpha_x, alpha_w, out):
             leave(c - 1, 1, scopy)
             leave(c - 1, 2, scopy)
             leave(c - 1, 3, scopy)
-            if c < 3:
-                sign_chunk(c + 1)
+            if c == 1:
+                sign_chunk(2)
             if c < 3:
                 for ob in range(OBS):
                     times_sign_w(c, ob)

@@ -166,8 +166,11 @@ def tile_pointwise_kernel(tc, x, weight, alpha_x, alpha_w, out):
         def quantise_x(c):
             quantise(xq[c][:], xs[c][:], flat(xg, c))
 
-        def quantise_x_part(c, lo, hi):
-            quantise(xq[c][:, lo:hi], xs[c][:, lo:hi], xg[c][:, lo:hi, :].rearrange("p w j -> p (w j)"))
+        def grow_part(c, lo, hi):
+            blow_up(flat(sg, c, lo, hi), flat(tmp, c, lo, hi))
+
+        def quantise_s_part(c, lo, hi):
+            quantise(sq[c][:, lo:hi], ss[c][:, lo:hi], flat(sg, c, lo, hi))
 
         def quantise_s(c):
             quantise(sq[c][:], ss[c][:], flat(sg, c))
@@ -194,11 +197,13 @@ def tile_pointwise_kernel(tc, x, weight, alpha_x, alpha_w, out):
         def times_w(c, ob):
             mx_pass(c, ob, wq, ws, sq, ss)
 
-        def leave(c, ob, copy):
-            copy(out=res[c][:, ob, :], in_=acc[(c, ob)][:])
-            b, lo = divmod(c * N, HW)
-            dram = out[b].rearrange("(m ob) h w -> m ob (h w)", ob=OBS)[:, :, lo : lo + N]
-            nc.sync.dma_start(out=dram[:, ob : ob + 1, :], in_=res[c][:, ob : ob + 1, :])
+        def leave(c, ob, copy, lo=0, hi=N):
+            copy(out=res[c][:, ob, lo:hi], in_=acc[(c, ob)][:, lo:hi])
+            b, first = divmod(c * N, HW)
+            dram = out[b].rearrange("(m ob) h w -> m ob (h w)", ob=OBS)
+            nc.sync.dma_start(
+                out=dram[:, ob : ob + 1, first + lo : first + hi], in_=res[c][:, ob : ob + 1, lo:hi]
+            )
 
         vcopy = nc.vector.tensor_copy
         scopy = nc.scalar.copy
@@ -243,14 +248,15 @@ def tile_pointwise_kernel(tc, x, weight, alpha_x, alpha_w, out):
                 if c > 1:
                     grow_chunk(c)
             else:
-                quantise_x_part(c, 0, HEAD)
-                grow_chunk(c)
-                quantise_x_part(c, HEAD, N)
-                quantise_s(c)
+                quantise_x(c)
+                grow_part(c, 0, HEAD)
+                grow_part(c, HEAD, N)
+                quantise_s_part(c, 0, HEAD)
+                quantise_s_part(c, HEAD, N)
             leave(c - 1, 0, scopy)
             leave(c - 1, 1, scopy)
             leave(c - 1, 2, scopy)
-            leave(c - 1, 3, scopy)
+            leave(c - 1, 3, vcopy if c == 3 else scopy)
             if c == 1:
                 sign_chunk(2)
             if c < 3:
@@ -261,13 +267,12 @@ def tile_pointwise_kernel(tc, x, weight, alpha_x, alpha_w, out):
                 for ob in range(OBS):
                     times_w(c, ob)
             else:
-                times_sign_w(3, 0)
-                times_sign_w(3, 1)
-                times_w(3, 0)
-                times_sign_w(3, 2)
-                times_w(3, 1)
-                times_sign_w(3, 3)
-                times_w(3, 2)
-                times_w(3, 3)
-        for ob in range(OBS):
-            leave(3, ob, (scopy, vcopy)[ob % 2])
+                for ob in range(OBS):
+                    times_sign_w(3, ob)
+                for ob in range(OBS):
+                    times_w(3, ob)
+        leave(3, 0, scopy, 0, HEAD)
+        leave(3, 0, scopy, HEAD, N)
+        leave(3, 1, vcopy)
+        leave(3, 2, scopy)
+        leave(3, 3, vcopy)

@@ -23,7 +23,7 @@ TINY = 2.0 ** -133
 UP_A = 2.0 ** 67
 UP_B = 2.0 ** 66
 
-VECTOR_SIGN = ((192, 256), (512, 512), (256, 512), (0, 512))
+VECTOR_SIGN = ((192, 256), (512, 512), (192, 512), (0, 512))
 HEAD = 256
 RUN = 8
 

from contextlib import ExitStack

import concourse.mybir as mybir
from concourse.masks import make_identity

FLOPS = 2 * 2 * 2 * 1024 * 512 * 512

BF16 = mybir.dt.bfloat16
F32 = mybir.dt.float32
U32 = mybir.dt.uint32
U8 = mybir.dt.uint8
FP8X4 = mybir.dt.float8_e4m3fn_x4
ALU = mybir.AluOpType
ACT = mybir.ActivationFunctionType

P = 128
PACK = 4
OBS = 4
HW = 1024
N = 512
CHUNKS = 4
TINY = 2.0 ** -133
UP_A = 2.0 ** 67
UP_B = 2.0 ** 66

VECTOR_SIGN = ((192, 256), (512, 512), (192, 512), (0, 512))
HEAD = 256
RUN = 8


def by_fours(grouped_ap, rows_ap):
    return (
        grouped_ap.rearrange("p (c i) t -> p c t i", i=RUN),
        rows_ap.rearrange("p t (c i) -> p c t i", i=RUN),
    )


def tile_pointwise_kernel(tc, x, weight, alpha_x, alpha_w, out):
    nc = tc.nc
    with ExitStack() as ctx:
        keep = ctx.enter_context(tc.tile_pool(name="keep", bufs=1))
        psum = ctx.enter_context(tc.psum_pool(name="psum", bufs=1))
        ctx.enter_context(tc.manual_schedule())

        ident = keep.tile([P, P], F32, name="ident")
        make_identity(nc, ident[:])

        pieces = ((0, 0, HEAD), (0, HEAD, N - HEAD), (1, 0, N), (2, 0, 2 * N))
        raw = {}
        w_sb = {}

        def load_x(i):
            c, lo, cols = pieces[i]
            b, first = divmod(c * N + lo, HW)
            raw[i] = keep.tile([P, PACK, cols], BF16, name="raw%d" % i)
            nc.sync.dma_start(
                out=raw[i][:],
                in_=x[b].rearrange("(p j) h w -> p j (h w)", j=PACK)[:, :, first : first + cols],
            )

        def load_w(pair):
            w_sb[pair] = keep.tile([P, 2, 512], BF16, name="w_sb%d" % pair)
            nc.sync.dma_start(
                out=w_sb[pair][:],
                in_=weight.rearrange("(p ob) c a b -> p ob (c a b)", ob=OBS)[:, 2 * pair : 2 * pair + 2, :],
            )

        load_x(0)
        load_x(1)
        load_w(0)
        load_w(1)
        load_x(2)
        load_x(3)

        chunks = range(CHUNKS)
        xg = [keep.tile([P, N, PACK], BF16, name="xg%d" % c, align_bytes=64) for c in chunks]
        sg = [keep.tile([P, N, PACK], BF16, name="sg%d" % c, align_bytes=64) for c in chunks]
        tmp = [keep.tile([P, N, PACK], BF16, name="tmp%d" % c, align_bytes=64) for c in chunks]
        xq = [keep.tile([P, N], U32, name="xq%d" % c, align_bytes=64) for c in chunks]
        xs = [keep.tile([P, N], U8, name="xs%d" % c, align_bytes=64) for c in chunks]
        sq = [keep.tile([P, N], U32, name="sq%d" % c, align_bytes=64) for c in chunks]
        ss = [keep.tile([P, N], U8, name="ss%d" % c, align_bytes=64) for c in chunks]
        res = [keep.tile([P, OBS, N], F32, name="res%d" % c) for c in chunks]

        wg = keep.tile([P, OBS * P * PACK], BF16, name="wg", align_bytes=64)
        swg = keep.tile([P, OBS * P * PACK], BF16, name="swg", align_bytes=64)
        wtmp = keep.tile([P, OBS * P * PACK], BF16, name="wtmp", align_bytes=64)
        wq = keep.tile([P, OBS * P], U32, name="wq", align_bytes=64)
        ws = keep.tile([P, OBS * P], U8, name="ws", align_bytes=64)
        swq = keep.tile([P, OBS * P], U32, name="swq", align_bytes=64)
        sws = keep.tile([P, OBS * P], U8, name="sws", align_bytes=64)
        wg_words = wg[:].bitcast(F32).rearrange("p (ob m u) -> p ob m u", ob=OBS, u=2)

        warm = keep.tile([P, N], BF16, name="warm")
        nc.vector.memset(warm[:], 0.0)

        wt = {}
        acc = {}
        opened = set()

        def new_bank(shape, name, k):
            return psum.tile(shape, F32, tag="bank%d" % (k % 8), name=name)

        def quantise(codes, scales, values):
            nc.vector.quantize_mx(out=codes.bitcast(FP8X4), scales=scales, in_=values)

        def clamp(dst, src):
            nc.vector.tensor_scalar(out=dst, in0=src, scalar1=-TINY, scalar2=TINY, op0=ALU.max, op1=ALU.min)

        def blow_up(dst, src):
            nc.vector.tensor_scalar(out=dst, in0=src, scalar1=UP_A, scalar2=UP_B, op0=ALU.mult, op1=ALU.mult)

        def flat(t, c, lo=0, hi=N):
            return t[c][:, lo:hi, :].rearrange("p w j -> p (w j)")

        def transpose_w(pair):
            words = w_sb[pair][:].rearrange("p ob c -> p (ob c)").bitcast(F32).rearrange(
                "p (ob q u) -> p ob q u", ob=2, u=2
            )
            wt[pair] = new_bank([P, 2, 2, P], "wt%d" % pair, pair)
            for i in range(2):
                for u in range(2):
                    nc.tensor.transpose(wt[pair][:, i, u, :], words[:, i, :, u], ident[:])

        warm_out = new_bank([P, N], "warm_out", 7)

        def warm_up(passes):
            for i in range(passes):
                nc.tensor.matmul(warm_out[:], lhsT=warm[:, :P], rhs=warm[:], start=True, stop=True)

        def exit_w(pair, copy):
            copy(out=wg_words[:, 2 * pair : 2 * pair + 2], in_=wt[pair][:].rearrange("p i u m -> p i m u"))

        def wcols(pair):
            return slice(pair * 2 * P, (pair + 1) * 2 * P)

        def wvals(pair):
            return slice(pair * 2 * P * PACK, (pair + 1) * 2 * P * PACK)

        def quantise_w(pair):
            quantise(wq[:, wcols(pair)], ws[:, wcols(pair)], wg[:, wvals(pair)])

        def quantise_sw(pair):
            quantise(swq[:, wcols(pair)], sws[:, wcols(pair)], swg[:, wvals(pair)])

        def regroup(c, i, dst_lo, src_lo, cols):
            dst, src = by_fours(xg[c][:, dst_lo : dst_lo + cols, :], raw[i][:, :, src_lo : src_lo + cols])
            nc.vector.tensor_copy(out=dst, in_=src)

        def sign(c, i, dst_lo, src_lo, cols):
            dst, src = by_fours(sg[c][:, dst_lo : dst_lo + cols, :], raw[i][:, :, src_lo : src_lo + cols])
            nc.scalar.activation(out=dst, in_=src, func=ACT.Sign)

        def regroup_chunk(c):
            regroup(c, min(c + 1, 3), 0, N * (c == 3), N)

        def sign_chunk(c):
            sign(c, min(c + 1, 3), 0, N * (c == 3), VECTOR_SIGN[c][0])

        def clamp_chunk(c):
            clamp(flat(tmp, c, *VECTOR_SIGN[c]), flat(xg, c, *VECTOR_SIGN[c]))

        def grow_chunk(c):
            blow_up(flat(sg, c, *VECTOR_SIGN[c]), flat(tmp, c, *VECTOR_SIGN[c]))

        def quantise_x(c):
            quantise(xq[c][:], xs[c][:], flat(xg, c))

        def grow_part(c, lo, hi):
            blow_up(flat(sg, c, lo, hi), flat(tmp, c, lo, hi))

        def quantise_s_part(c, lo, hi):
            quantise(sq[c][:, lo:hi], ss[c][:, lo:hi], flat(sg, c, lo, hi))

        def quantise_s(c):
            quantise(sq[c][:], ss[c][:], flat(sg, c))

        def mx_pass(c, ob, w_codes, w_scales, x_codes, x_scales):
            cols = slice(ob * P, (ob + 1) * P)
            first = (c, ob) not in opened
            opened.add((c, ob))
            if first:
                acc[(c, ob)] = new_bank([P, N], "acc%d_%d" % (c, ob), 2 + OBS * c + ob)
            nc.tensor.matmul_mx(
                out=acc[(c, ob)][:],
                lhsT=w_codes[:, cols].bitcast(FP8X4),
                lhsT_scale=w_scales[:, cols],
                rhs=x_codes[c][:].bitcast(FP8X4),
                rhs_scale=x_scales[c][:],
                start=first,
                stop=not first,
            )

        def times_sign_w(c, ob):
            mx_pass(c, ob, swq, sws, xq, xs)

        def times_w(c, ob):
            mx_pass(c, ob, wq, ws, sq, ss)

        def leave(c, ob, copy, lo=0, hi=N):
            copy(out=res[c][:, ob, lo:hi], in_=acc[(c, ob)][:, lo:hi])
            b, first = divmod(c * N, HW)
            dram = out[b].rearrange("(m ob) h w -> m ob (h w)", ob=OBS)
            nc.sync.dma_start(
                out=dram[:, ob : ob + 1, first + lo : first + hi], in_=res[c][:, ob : ob + 1, lo:hi]
            )

        vcopy = nc.vector.tensor_copy
        scopy = nc.scalar.copy

        warm_up(6)
        regroup(0, 0, 0, 0, HEAD)
        sign(0, 0, 0, 0, VECTOR_SIGN[0][0])
        regroup(0, 1, HEAD, 0, N - HEAD)
        sign(0, 1, HEAD, 0, N - HEAD)
        transpose_w(0)
        transpose_w(1)
        warm_up(3)
        clamp_chunk(0)
        quantise_x(0)
        grow_chunk(0)
        exit_w(0, scopy)
        exit_w(1, scopy)
        quantise_s(0)
        clamp(wtmp[:, wvals(0)], wg[:, wvals(0)])
        nc.scalar.activation(out=swg[:, wvals(1)], in_=wg[:, wvals(1)], func=ACT.Sign)
        quantise_w(0)
        blow_up(swg[:, wvals(0)], wtmp[:, wvals(0)])
        times_w(0, 0)
        times_w(0, 1)
        quantise_w(1)
        quantise_sw(0)
        sign_chunk(1)
        times_sign_w(0, 0)
        times_sign_w(0, 1)
        regroup_chunk(1)
        times_w(0, 2)
        times_w(0, 3)
        quantise_sw(1)
        times_sign_w(0, 2)
        times_sign_w(0, 3)

        for c in range(1, CHUNKS):
            if c > 1:
                clamp_chunk(c)
            if c < 3:
                quantise_x(c)
                if c > 1:
                    grow_chunk(c)
            else:
                quantise_x(c)
                grow_part(c, 0, HEAD)
                grow_part(c, HEAD, N)
                quantise_s_part(c, 0, HEAD)
                quantise_s_part(c, HEAD, N)
            leave(c - 1, 0, scopy)
            leave(c - 1, 1, scopy)
            leave(c - 1, 2, scopy)
            leave(c - 1, 3, vcopy if c == 3 else scopy)
            if c == 1:
                sign_chunk(2)
            if c < 3:
                for ob in range(OBS):
                    times_sign_w(c, ob)
                regroup_chunk(c + 1)
                quantise_s(c)
                for ob in range(OBS):
                    times_w(c, ob)
            else:
                for ob in range(OBS):
                    times_sign_w(3, ob)
                for ob in range(OBS):
                    times_w(3, ob)
        leave(3, 0, scopy, 0, HEAD)
        leave(3, 0, scopy, HEAD, N)
        leave(3, 1, vcopy)
        leave(3, 2, scopy)
        leave(3, 3, vcopy)
